import numpy as np
import ml_dtypes


def mxq(x, axis, fmt="e4m3"):
    dtype, down = {"e4m3": (ml_dtypes.float8_e4m3fn, 7), "e5m2": (ml_dtypes.float8_e5m2, 14)}[fmt]
    v = np.moveaxis(np.asarray(x, np.float32).astype(ml_dtypes.bfloat16).astype(np.float64), axis, -1)
    blocks = v.reshape(v.shape[:-1] + (-1, 32))
    amax = np.abs(blocks).max(-1, keepdims=True)
    byte = np.maximum(np.where(amax > 0, np.frexp(amax)[1] - 1 + 127, 0) - down, 1)
    scale = np.exp2(byte - 127.0)
    codes = (blocks / scale).astype(np.float32).astype(dtype).astype(np.float64)
    return np.moveaxis((codes * scale).reshape(v.shape), -1, axis)


WIDE = False


def mx_kscale(k):
    if not WIDE:
        return np.ones(k)
    levels = np.array([10, -10, 5, -5, 0])
    a = np.random.permutation(np.resize(levels, k // 512 * 4)).reshape(k // 512, 4)
    idx = np.arange(k)
    return np.exp2(a[idx // 512, idx % 128 // 32])


BF16 = ml_dtypes.bfloat16


def bf(x):
    return np.asarray(x, np.float32).astype(BF16)


def f64(x):
    return np.asarray(x).astype(np.float64)


E2M1 = np.array([0.0, 0.5, 1.0, 1.5, 2.0, 3.0, 4.0, 6.0, -0.0, -0.5, -1.0, -1.5, -2.0, -3.0, -4.0, -6.0])


def pack_weight(w, fmt):
    k, n = w.shape
    w = f64(bf(w)).reshape(k // 32, 32, n)
    amax = np.abs(w).max(1)
    if fmt == "e4m3":
        byte = np.frexp(amax)[1] - 1 + 127 - 7
    else:
        mant, ex = np.frexp(amax / 6.0)
        byte = np.where(mant > 0.5, ex, ex - 1) + 127
    byte = np.clip(np.where(amax > 0, byte, 1), 1, 254)
    scaled = (w * np.exp2(127.0 - byte)[:, None, :]).reshape(k, n).astype(np.float32)
    by_word = np.ascontiguousarray(scaled.reshape(k // 512, 128, 4, n).transpose(0, 1, 3, 2))
    if fmt == "e4m3":
        words = by_word.astype(ml_dtypes.float8_e4m3fn).view(np.uint8)
    else:
        c = by_word.astype(ml_dtypes.float4_e2m1fn).view(np.uint8) & 0xF
        words = c[..., 0::2] | (c[..., 1::2] << 4)
    return np.ascontiguousarray(words), np.ascontiguousarray(byte.astype(np.uint8).reshape(k // 512, 16, n))


def unpack_weight(words, scales, fmt):
    g, p, n, _ = words.shape
    if fmt == "e4m3":
        vals = np.ascontiguousarray(words).view(ml_dtypes.float8_e4m3fn).astype(np.float64)
    else:
        nib = np.empty((g, p, n, 4), np.uint8)
        nib[..., 0::2] = words & 0xF
        nib[..., 1::2] = words >> 4
        vals = E2M1[nib]
    vals = vals * np.repeat(np.exp2(scales.astype(np.float64) - 127.0), 8, axis=1)[..., None]
    return vals.transpose(0, 1, 3, 2).reshape(g * 512, n)

def pack4(w):
    words, scales = pack_weight(w, "e2m1")
    return words.reshape(words.shape[0], 128, -1), scales


def unpack4(words, scales):
    return unpack_weight(words.reshape(words.shape[0], 128, -1, 2), scales, "e2m1")


B, IN, H, Z, G = 512, 1024, 1024, 256, 4


def setup_inputs():
    s = mx_kscale(IN)
    src_x = bf(np.random.standard_normal((B, IN)) * s)
    zx = bf(np.random.standard_normal((B, G, Z)))
    dx_w = bf(np.random.standard_normal((G, H, Z)) / np.sqrt(Z))
    w_x = np.random.standard_normal((G, H, IN)) / np.sqrt(IN) / s
    cat = np.ascontiguousarray(w_x.swapaxes(1, 2)).reshape(-1, H)
    words, scales = pack4(cat)
    return {"src_x": src_x,
            "zx": zx,
            "dx_w": dx_w,
            "w_x_words": words,
            "w_x_scales": scales}


def reference(src_x, zx, dx_w, w_x_words, w_x_scales):
    d_x = (f64(zx).transpose(1, 0, 2) @ f64(dx_w).transpose(0, 2, 1)).transpose(1, 0, 2)
    wx = (mxq(f64(src_x), 1, "e4m3") @ unpack4(w_x_words, w_x_scales).reshape(G, IN, H).transpose(1, 0, 2).reshape(IN, G * H)).reshape(B, G, H)
    return d_x * wx

@@ -1,0 +1,192 @@
+from contextlib import ExitStack
+
+import concourse.mybir as mybir
+from concourse.masks import make_identity
+
+F32 = mybir.dt.float32
+BF16 = mybir.dt.bfloat16
+I32 = mybir.dt.int32
+U32 = mybir.dt.uint32
+U8 = mybir.dt.uint8
+FP8X4 = mybir.dt.float8_e4m3fn_x4
+FP4X4 = mybir.dt.float4_e2m1fn_x4
+
+P = 128
+BATCH, IN, H, Z, GATES = 512, 1024, 1024, 256, 4
+BATCH_TILES = BATCH // P
+K_PASS = 4 * P
+PASSES = IN // K_PASS
+BANK = 512
+HALVES = H // BANK
+PAIR = 2
+BLOCKS = 4
+DXW_LOW, ZX, DXW_HIGH = 0, 1, 2
+PIECES = 3
+
+FLOPS = 2 * BATCH * GATES * H * (IN + Z)
+
+
+def tile_metalstmcell_pa_e_kernel(tc, src_x, zx, dx_w, w_x_words, w_x_scales, out):
+    nc = tc.nc
+    with ExitStack() as ctx:
+        ctx.enter_context(tc.manual_schedule())
+        keep = ctx.enter_context(tc.tile_pool(name="keep", bufs=1))
+        d_pool = ctx.enter_context(tc.tile_pool(name="d_pool", bufs=BATCH_TILES + 2))
+        res_pool = ctx.enter_context(tc.tile_pool(name="res_pool", bufs=4))
+        flip_psum = ctx.enter_context(tc.psum_pool(name="flip_psum", bufs=2))
+        d_psum = ctx.enter_context(tc.psum_pool(name="d_psum", bufs=3))
+        w_psum = ctx.enter_context(tc.psum_pool(name="w_psum", bufs=3))
+
+        ident = keep.tile([P, P], F32, name="ident")
+        x_raw = [keep.tile([P, IN], BF16, name="x_raw%d" % bt) for bt in range(BATCH_TILES)]
+        x_grouped = [
+            keep.tile([P, PASSES * P * 4], BF16, name="x_grouped%d" % bt, align_bytes=64)
+            for bt in range(BATCH_TILES)
+        ]
+        x_codes = [
+            keep.tile([P, PASSES * P], U32, name="x_codes%d" % bt, align_bytes=64)
+            for bt in range(BATCH_TILES)
+        ]
+        x_scales = [
+            keep.tile([P, PASSES * P], U8, name="x_scales%d" % bt, align_bytes=64)
+            for bt in range(BATCH_TILES)
+        ]
+        piece_raw = [
+            [keep.tile([P, BLOCKS, Z], BF16, name="piece_raw%d_%d" % (g, i)) for i in range(PIECES)]
+            for g in range(GATES)
+        ]
+        piece_flipped = [
+            [
+                keep.tile([P, BLOCKS * P, PAIR], BF16, name="piece_flipped%d_%d" % (g, i))
+                for i in range(PIECES)
+            ]
+            for g in range(GATES)
+        ]
+        w_words = [
+            keep.tile([P, PASSES, 2 * H], U8, name="w_words%d" % g, align_bytes=64)
+            for g in range(GATES)
+        ]
+        w_scales = keep.tile([P, GATES * PASSES, H], U8, name="w_scales", align_bytes=64)
+
+        nc.vector.memset(w_scales[:].bitcast(I32), 0)
+        make_identity(nc, ident[:])
+
+        def load_piece(g, i):
+            rows = zx[:, g, :] if i == ZX else dx_w[g, (i // 2) * BANK : (i // 2 + 1) * BANK, :]
+            nc.sync.dma_start(
+                out=piece_raw[g][i][:], in_=rows.rearrange("(j p) z -> p j z", p=P)
+            )
+
+        for i in range(PIECES):
+            load_piece(0, i)
+        for bt in range(BATCH_TILES):
+            nc.sync.dma_start(out=x_raw[bt][:], in_=src_x[bt * P : (bt + 1) * P, :])
+            if bt < PIECES:
+                load_piece(1, bt)
+        scale_rows = w_x_scales.bitcast(I32).rearrange("c q n -> q c n")
+        for q in range(8):
+            first = 32 * (q // 4) + q % 4
+            nc.sync.dma_start(
+                out=w_scales[:].bitcast(I32)[first : P : 64], in_=scale_rows[q : 16 : 8]
+            )
+        for g in range(GATES):
+            nc.sync.dma_start(
+                out=w_words[g][:].bitcast(I32),
+                in_=w_x_words.bitcast(I32)[g * PASSES : (g + 1) * PASSES].rearrange("c p n -> p c n"),
+            )
+            if g + 2 < GATES:
+                for i in range(PIECES):
+                    load_piece(g + 2, i)
+
+        def flip_of_x(bt):
+            words = x_raw[bt][:].bitcast(F32)
+            blocks = [
+                words[:, c * (K_PASS // PAIR) + u : (c + 1) * (K_PASS // PAIR) : 2]
+                for c in range(PASSES)
+                for u in range(2)
+            ]
+
+            def keep_bank(bank):
+                nc.vector.tensor_copy(
+                    out=x_grouped[bt][:].bitcast(F32).rearrange("p (c r u) -> p c r u", c=PASSES, u=2),
+                    in_=bank[:].rearrange("p (c u) r -> p c r u", u=2),
+                )
+                nc.vector.quantize_mx(
+                    out=x_codes[bt][:].bitcast(FP8X4), scales=x_scales[bt][:], in_=x_grouped[bt][:]
+                )
+
+            return blocks, keep_bank
+
+        def flip_of_piece(g, i):
+            words = piece_raw[g][i][:].bitcast(F32)
+            blocks = [words[:, j, :] for j in range(BLOCKS)]
+
+            def keep_bank(bank):
+                nc.scalar.copy(
+                    out=piece_flipped[g][i][:].rearrange("p r e -> p (r e)"),
+                    in_=bank[:].rearrange("p j r -> p (j r)").bitcast(BF16),
+                )
+
+            return blocks, keep_bank
+
+        def transposes(bank, blocks, which):
+            for j in which:
+                nc.tensor.transpose(bank[:, j, :], blocks[j], ident[:])
+
+        d_x = {}
+
+        def plain_run(g, bt, flips):
+            d_x[(g, bt)] = d_pool.tile([P, H], F32, name="d_x")
+            for hh in range(HALVES):
+                cols = slice(hh * BANK, (hh + 1) * BANK)
+                d_acc = d_psum.tile([P, BANK], F32, name="d_acc")
+                if hh < len(flips):
+                    blocks, keep_bank = flips[hh]
+                    bank = flip_psum.tile([P, BLOCKS, P], F32, name="bank")
+                for e in range(PAIR):
+                    nc.tensor.matmul(
+                        d_acc[:],
+                        lhsT=piece_flipped[g][ZX][:, bt * P : (bt + 1) * P, e],
+                        rhs=piece_flipped[g][2 * hh][:, :, e],
+                        start=(e == 0),
+                        stop=(e == PAIR - 1),
+                    )
+                    if hh < len(flips):
+                        transposes(bank, blocks, (2 * e, 2 * e + 1))
+                nc.scalar.copy(out=d_x[(g, bt)][:, cols], in_=d_acc[:])
+                if hh < len(flips):
+                    keep_bank(bank)
+
+        def mx_run(g, bt):
+            res = res_pool.tile([P, H], F32, name="res")
+            for hh in range(HALVES):
+                cols = slice(hh * BANK, (hh + 1) * BANK)
+                w_acc = w_psum.tile([P, BANK], F32, name="w_acc")
+                for c in range(PASSES):
+                    nc.tensor.matmul_mx(
+                        out=w_acc[:],
+                        lhsT=x_codes[bt][:, c * P : (c + 1) * P].bitcast(FP8X4),
+                        lhsT_scale=x_scales[bt][:, c * P : (c + 1) * P],
+                        rhs=w_words[g][:, c, 2 * hh * BANK : 2 * (hh + 1) * BANK].bitcast(FP4X4),
+                        rhs_scale=w_scales[:, g * PASSES + c, cols],
+                        start=(c == 0),
+                        stop=(c == PASSES - 1),
+                    )
+                nc.vector.tensor_tensor(
+                    out=res[:, cols], in0=w_acc[:], in1=d_x[(g, bt)][:, cols], op=mybir.AluOpType.mult
+                )
+            nc.sync.dma_start(out=out[bt * P : (bt + 1) * P, g, :], in_=res[:])
+
+        for i in range(PIECES):
+            blocks, keep_bank = flip_of_piece(0, i)
+            bank = flip_psum.tile([P, BLOCKS, P], F32, name="bank")
+            transposes(bank, blocks, range(BLOCKS))
+            keep_bank(bank)
+        for bt in range(BATCH_TILES):
+            plain_run(0, bt, [flip_of_x(bt)] + [flip_of_piece(1, i) for i in range(PIECES)][bt : bt + 1])
+        for g in range(GATES):
+            for bt in range(BATCH_TILES):
+                mx_run(g, bt)
+                if g + 1 < GATES:
+                    carried = [flip_of_piece(g + 2, i) for i in range(PIECES)] if g + 2 < GATES else []
+                    plain_run(g + 1, bt, carried[bt : bt + 1])

@@ -18,6 +18,8 @@ K_PASS = 4 * P
 PASSES = IN // K_PASS
 BANK = 512
 HALVES = H // BANK
+RUN = 2
+RUNS = HALVES * BATCH_TILES // RUN
 PAIR = 2
 BLOCKS = 4
 DXW_LOW, ZX, DXW_HIGH = 0, 1, 2
@@ -31,11 +33,9 @@ def tile_metalstmcell_pa_e_kernel(tc, src_x, zx, dx_w, w_x_words, w_x_scales, ou
     with ExitStack() as ctx:
         ctx.enter_context(tc.manual_schedule())
         keep = ctx.enter_context(tc.tile_pool(name="keep", bufs=1))
-        d_pool = ctx.enter_context(tc.tile_pool(name="d_pool", bufs=BATCH_TILES + 2))
-        res_pool = ctx.enter_context(tc.tile_pool(name="res_pool", bufs=4))
-        flip_psum = ctx.enter_context(tc.psum_pool(name="flip_psum", bufs=2))
-        d_psum = ctx.enter_context(tc.psum_pool(name="d_psum", bufs=3))
-        w_psum = ctx.enter_context(tc.psum_pool(name="w_psum", bufs=3))
+        d_pool = ctx.enter_context(tc.tile_pool(name="d_pool", bufs=(RUNS + 2) * RUN))
+        res_pool = ctx.enter_context(tc.tile_pool(name="res_pool", bufs=8))
+        psum = ctx.enter_context(tc.psum_pool(name="psum", bufs=8))
 
         ident = keep.tile([P, P], F32, name="ident")
         x_raw = [keep.tile([P, IN], BF16, name="x_raw%d" % bt) for bt in range(BATCH_TILES)]
@@ -81,8 +81,8 @@ def tile_metalstmcell_pa_e_kernel(tc, src_x, zx, dx_w, w_x_words, w_x_scales, ou
             load_piece(0, i)
         for bt in range(BATCH_TILES):
             nc.sync.dma_start(out=x_raw[bt][:], in_=src_x[bt * P : (bt + 1) * P, :])
-            if bt < PIECES:
-                load_piece(1, bt)
+        for i in range(PIECES):
+            load_piece(1, i)
         scale_rows = w_x_scales.bitcast(I32).rearrange("c q n -> q c n")
         for q in range(8):
             first = 32 * (q // 4) + q % 4
@@ -122,7 +122,7 @@ def tile_metalstmcell_pa_e_kernel(tc, src_x, zx, dx_w, w_x_words, w_x_scales, ou
             blocks = [words[:, j, :] for j in range(BLOCKS)]
 
             def keep_bank(bank):
-                nc.scalar.copy(
+                nc.vector.tensor_copy(
                     out=piece_flipped[g][i][:].rearrange("p r e -> p (r e)"),
                     in_=bank[:].rearrange("p j r -> p (j r)").bitcast(BF16),
                 )
@@ -133,16 +133,18 @@ def tile_metalstmcell_pa_e_kernel(tc, src_x, zx, dx_w, w_x_words, w_x_scales, ou
             for j in which:
                 nc.tensor.transpose(bank[:, j, :], blocks[j], ident[:])
 
+        def banks_of_run(r):
+            hh, group = divmod(r, BATCH_TILES // RUN)
+            return [(hh, group * RUN + i) for i in range(RUN)]
+
         d_x = {}
 
-        def plain_run(g, bt, flips):
-            d_x[(g, bt)] = d_pool.tile([P, H], F32, name="d_x")
-            for hh in range(HALVES):
-                cols = slice(hh * BANK, (hh + 1) * BANK)
-                d_acc = d_psum.tile([P, BANK], F32, name="d_acc")
-                if hh < len(flips):
-                    blocks, keep_bank = flips[hh]
-                    bank = flip_psum.tile([P, BLOCKS, P], F32, name="bank")
+        def plain_run(g, r, flips):
+            for i, (hh, bt) in enumerate(banks_of_run(r)):
+                d_acc = psum.tile([P, BANK], F32, name="d_acc", tag="bank")
+                if i < len(flips):
+                    blocks, keep_bank = flips[i]
+                    bank = psum.tile([P, BLOCKS, P], F32, name="flip_bank", tag="bank")
                 for e in range(PAIR):
                     nc.tensor.matmul(
                         d_acc[:],
@@ -151,17 +153,17 @@ def tile_metalstmcell_pa_e_kernel(tc, src_x, zx, dx_w, w_x_words, w_x_scales, ou
                         start=(e == 0),
                         stop=(e == PAIR - 1),
                     )
-                    if hh < len(flips):
+                    if i < len(flips):
                         transposes(bank, blocks, (2 * e, 2 * e + 1))
-                nc.scalar.copy(out=d_x[(g, bt)][:, cols], in_=d_acc[:])
-                if hh < len(flips):
+                d_x[(g, hh, bt)] = d_pool.tile([P, BANK], F32, name="d_x")
+                nc.scalar.copy(out=d_x[(g, hh, bt)][:], in_=d_acc[:])
+                if i < len(flips):
                     keep_bank(bank)
 
-        def mx_run(g, bt):
-            res = res_pool.tile([P, H], F32, name="res")
-            for hh in range(HALVES):
+        def mx_run(g, r):
+            for hh, bt in banks_of_run(r):
                 cols = slice(hh * BANK, (hh + 1) * BANK)
-                w_acc = w_psum.tile([P, BANK], F32, name="w_acc")
+                w_acc = psum.tile([P, BANK], F32, name="w_acc", tag="bank")
                 for c in range(PASSES):
                     nc.tensor.matmul_mx(
                         out=w_acc[:],
@@ -172,21 +174,27 @@ def tile_metalstmcell_pa_e_kernel(tc, src_x, zx, dx_w, w_x_words, w_x_scales, ou
                         start=(c == 0),
                         stop=(c == PASSES - 1),
                     )
+                res = res_pool.tile([P, BANK], F32, name="res")
                 nc.vector.tensor_tensor(
-                    out=res[:, cols], in0=w_acc[:], in1=d_x[(g, bt)][:, cols], op=mybir.AluOpType.mult
+                    out=res[:], in0=w_acc[:], in1=d_x[(g, hh, bt)][:], op=mybir.AluOpType.mult
                 )
-            nc.sync.dma_start(out=out[bt * P : (bt + 1) * P, g, :], in_=res[:])
+                nc.sync.dma_start(out=out[bt * P : (bt + 1) * P, g, cols], in_=res[:])
 
-        for i in range(PIECES):
+        for i in (DXW_LOW, ZX):
             blocks, keep_bank = flip_of_piece(0, i)
-            bank = flip_psum.tile([P, BLOCKS, P], F32, name="bank")
+            bank = psum.tile([P, BLOCKS, P], F32, name="flip_bank", tag="bank")
             transposes(bank, blocks, range(BLOCKS))
             keep_bank(bank)
-        for bt in range(BATCH_TILES):
-            plain_run(0, bt, [flip_of_x(bt)] + [flip_of_piece(1, i) for i in range(PIECES)][bt : bt + 1])
+        early = (
+            [flip_of_piece(0, DXW_HIGH)]
+            + [flip_of_x(bt) for bt in range(BATCH_TILES)]
+            + [flip_of_piece(1, i) for i in range(PIECES)]
+        )
+        for r in range(RUNS):
+            plain_run(0, r, early[r * RUN : (r + 1) * RUN])
         for g in range(GATES):
-            for bt in range(BATCH_TILES):
-                mx_run(g, bt)
+            for r in range(RUNS):
+                mx_run(g, r)
                 if g + 1 < GATES:
-                    carried = [flip_of_piece(g + 2, i) for i in range(PIECES)] if g + 2 < GATES else []
-                    plain_run(g + 1, bt, carried[bt : bt + 1])
+                    later = [flip_of_piece(g + 2, i) for i in range(PIECES)] if g + 2 < GATES else []
+                    plain_run(g + 1, r, later[r : r + 1])

@@ -66,9 +66,12 @@ def tile_metalstmcell_pa_e_kernel(tc, src_x, zx, dx_w, w_x_words, w_x_scales, ou
             keep.tile([P, PASSES, 2 * H], U8, name="w_words%d" % g, align_bytes=64)
             for g in range(GATES)
         ]
-        w_scales = keep.tile([P, GATES * PASSES, H], U8, name="w_scales", align_bytes=64)
+        w_scales = [
+            keep.tile([P, PASSES, H], U8, name="w_scales%d" % g, align_bytes=64) for g in range(GATES)
+        ]
 
-        nc.vector.memset(w_scales[:].bitcast(I32), 0)
+        for g in range(GATES):
+            nc.vector.memset(w_scales[g][:].bitcast(I32), 0)
         make_identity(nc, ident[:])
 
         def load_piece(g, i):
@@ -77,26 +80,39 @@ def tile_metalstmcell_pa_e_kernel(tc, src_x, zx, dx_w, w_x_words, w_x_scales, ou
                 out=piece_raw[g][i][:], in_=rows.rearrange("(j p) z -> p j z", p=P)
             )
 
-        for i in range(PIECES):
-            load_piece(0, i)
-        for bt in range(BATCH_TILES):
-            nc.sync.dma_start(out=x_raw[bt][:], in_=src_x[bt * P : (bt + 1) * P, :])
-        for i in range(PIECES):
-            load_piece(1, i)
         scale_rows = w_x_scales.bitcast(I32).rearrange("c q n -> q c n")
-        for q in range(8):
-            first = 32 * (q // 4) + q % 4
-            nc.sync.dma_start(
-                out=w_scales[:].bitcast(I32)[first : P : 64], in_=scale_rows[q : 16 : 8]
-            )
-        for g in range(GATES):
+
+        def load_scales(g):
+            for r in range(4):
+                nc.sync.dma_start(
+                    out=w_scales[g][:].bitcast(I32)[r : P : 32],
+                    in_=scale_rows[r : 16 : 4, g * PASSES : (g + 1) * PASSES],
+                )
+
+        def load_words(g):
             nc.sync.dma_start(
                 out=w_words[g][:].bitcast(I32),
                 in_=w_x_words.bitcast(I32)[g * PASSES : (g + 1) * PASSES].rearrange("c p n -> p c n"),
             )
-            if g + 2 < GATES:
-                for i in range(PIECES):
-                    load_piece(g + 2, i)
+
+        for i in range(PIECES):
+            load_piece(0, i)
+        for bt in range(BATCH_TILES):
+            nc.sync.dma_start(out=x_raw[bt][:], in_=src_x[bt * P : (bt + 1) * P, :])
+        load_piece(1, DXW_LOW)
+        load_piece(1, ZX)
+        load_scales(0)
+        load_words(0)
+        load_piece(1, DXW_HIGH)
+        for i in range(PIECES):
+            load_piece(2, i)
+        for g in range(1, GATES):
+            load_scales(g)
+        load_words(1)
+        for i in range(PIECES):
+            load_piece(3, i)
+        load_words(2)
+        load_words(3)
 
         def flip_of_x(bt):
             words = x_raw[bt][:].bitcast(F32)
@@ -170,7 +186,7 @@ def tile_metalstmcell_pa_e_kernel(tc, src_x, zx, dx_w, w_x_words, w_x_scales, ou
                         lhsT=x_codes[bt][:, c * P : (c + 1) * P].bitcast(FP8X4),
                         lhsT_scale=x_scales[bt][:, c * P : (c + 1) * P],
                         rhs=w_words[g][:, c, 2 * hh * BANK : 2 * (hh + 1) * BANK].bitcast(FP4X4),
-                        rhs_scale=w_scales[:, g * PASSES + c, cols],
+                        rhs_scale=w_scales[g][:, c, cols],
                         start=(c == 0),
                         stop=(c == PASSES - 1),
                     )
@@ -188,13 +204,17 @@ def tile_metalstmcell_pa_e_kernel(tc, src_x, zx, dx_w, w_x_words, w_x_scales, ou
         early = (
             [flip_of_piece(0, DXW_HIGH)]
             + [flip_of_x(bt) for bt in range(BATCH_TILES)]
-            + [flip_of_piece(1, i) for i in range(PIECES)]
+            + [flip_of_piece(1, DXW_LOW), flip_of_piece(1, ZX)]
         )
         for r in range(RUNS):
             plain_run(0, r, early[r * RUN : (r + 1) * RUN])
+        later = [flip_of_piece(1, DXW_HIGH)] + [
+            flip_of_piece(g, i) for g in range(2, GATES) for i in range(PIECES)
+        ]
+        done = 0
         for g in range(GATES):
             for r in range(RUNS):
                 mx_run(g, r)
                 if g + 1 < GATES:
-                    later = [flip_of_piece(g + 2, i) for i in range(PIECES)] if g + 2 < GATES else []
-                    plain_run(g + 1, r, later[r : r + 1])
+                    plain_run(g + 1, r, later[done : done + 1])
+                    done += 1

@@ -24,6 +24,8 @@ PAIR = 2
 BLOCKS = 4
 DXW_LOW, ZX, DXW_HIGH = 0, 1, 2
 PIECES = 3
+WARM_FIRST = 3
+WARM_BETWEEN = 1
 
 FLOPS = 2 * BATCH * GATES * H * (IN + Z)
 
@@ -70,6 +72,8 @@ def tile_metalstmcell_pa_e_kernel(tc, src_x, zx, dx_w, w_x_words, w_x_scales, ou
             keep.tile([P, PASSES, H], U8, name="w_scales%d" % g, align_bytes=64) for g in range(GATES)
         ]
 
+        warm = keep.tile([P, BANK], BF16, name="warm")
+        nc.vector.memset(warm[:], 0.0)
         for g in range(GATES):
             nc.vector.memset(w_scales[g][:].bitcast(I32), 0)
         make_identity(nc, ident[:])
@@ -196,11 +200,19 @@ def tile_metalstmcell_pa_e_kernel(tc, src_x, zx, dx_w, w_x_words, w_x_scales, ou
                 )
                 nc.sync.dma_start(out=out[bt * P : (bt + 1) * P, g, cols], in_=res[:])
 
+        warm_bank = psum.tile([P, BANK], F32, name="warm_bank", tag="bank")
+
+        def warm_up(n):
+            for i_warm in range(n):
+                nc.tensor.matmul(warm_bank[:], lhsT=warm[:, 0:P], rhs=warm[:], start=True, stop=True)
+
+        warm_up(WARM_FIRST)
         for i in (DXW_LOW, ZX):
             blocks, keep_bank = flip_of_piece(0, i)
             bank = psum.tile([P, BLOCKS, P], F32, name="flip_bank", tag="bank")
             transposes(bank, blocks, range(BLOCKS))
             keep_bank(bank)
+            warm_up(WARM_BETWEEN)
         early = (
             [flip_of_piece(0, DXW_HIGH)]
             + [flip_of_x(bt) for bt in range(BATCH_TILES)]

@@ -24,8 +24,15 @@ PAIR = 2
 BLOCKS = 4
 DXW_LOW, ZX, DXW_HIGH = 0, 1, 2
 PIECES = 3
+EARLY_X = 2
 WARM_FIRST = 3
 WARM_BETWEEN = 1
+FIRST_PARTS = (
+    (DXW_LOW, 0, 2, "vector"),
+    (DXW_LOW, 2, 2, "scalar"),
+    (ZX, 0, 1, "vector"),
+    (ZX, 1, 3, "vector"),
+)
 
 FLOPS = 2 * BATCH * GATES * H * (IN + Z)
 
@@ -36,7 +43,7 @@ def tile_metalstmcell_pa_e_kernel(tc, src_x, zx, dx_w, w_x_words, w_x_scales, ou
         ctx.enter_context(tc.manual_schedule())
         keep = ctx.enter_context(tc.tile_pool(name="keep", bufs=1))
         d_pool = ctx.enter_context(tc.tile_pool(name="d_pool", bufs=(RUNS + 2) * RUN))
-        res_pool = ctx.enter_context(tc.tile_pool(name="res_pool", bufs=8))
+        res_pool = ctx.enter_context(tc.tile_pool(name="res_pool", bufs=16))
         psum = ctx.enter_context(tc.psum_pool(name="psum", bufs=8))
 
         ident = keep.tile([P, P], F32, name="ident")
@@ -78,10 +85,11 @@ def tile_metalstmcell_pa_e_kernel(tc, src_x, zx, dx_w, w_x_words, w_x_scales, ou
             nc.vector.memset(w_scales[g][:].bitcast(I32), 0)
         make_identity(nc, ident[:])
 
-        def load_piece(g, i):
+        def load_piece(g, i, first=0, count=BLOCKS):
             rows = zx[:, g, :] if i == ZX else dx_w[g, (i // 2) * BANK : (i // 2 + 1) * BANK, :]
             nc.sync.dma_start(
-                out=piece_raw[g][i][:], in_=rows.rearrange("(j p) z -> p j z", p=P)
+                out=piece_raw[g][i][:, first : first + count, :],
+                in_=rows.rearrange("(j p) z -> p j z", p=P)[:, first : first + count, :],
             )
 
         scale_rows = w_x_scales.bitcast(I32).rearrange("c q n -> q c n")
@@ -93,20 +101,30 @@ def tile_metalstmcell_pa_e_kernel(tc, src_x, zx, dx_w, w_x_words, w_x_scales, ou
                     in_=scale_rows[r : 16 : 4, g * PASSES : (g + 1) * PASSES],
                 )
 
-        def load_words(g):
+        def load_words(g, first_half=0, halves=HALVES):
+            low, high = first_half * BANK // 2, (first_half + halves) * BANK // 2
             nc.sync.dma_start(
-                out=w_words[g][:].bitcast(I32),
-                in_=w_x_words.bitcast(I32)[g * PASSES : (g + 1) * PASSES].rearrange("c p n -> p c n"),
+                out=w_words[g][:].bitcast(I32)[:, :, low:high],
+                in_=w_x_words.bitcast(I32)[g * PASSES : (g + 1) * PASSES, :, low:high].rearrange(
+                    "c p n -> p c n"
+                ),
             )
 
-        for i in range(PIECES):
-            load_piece(0, i)
-        for bt in range(BATCH_TILES):
+        def load_x(bt):
             nc.sync.dma_start(out=x_raw[bt][:], in_=src_x[bt * P : (bt + 1) * P, :])
+
+        for i, first, count, copy in FIRST_PARTS:
+            load_piece(0, i, first, count)
+        load_piece(0, DXW_HIGH)
+        for bt in range(EARLY_X):
+            load_x(bt)
         load_piece(1, DXW_LOW)
         load_piece(1, ZX)
         load_scales(0)
-        load_words(0)
+        for hh in range(HALVES):
+            load_words(0, hh, 1)
+        for bt in range(EARLY_X, BATCH_TILES):
+            load_x(bt)
         load_piece(1, DXW_HIGH)
         for i in range(PIECES):
             load_piece(2, i)
@@ -127,15 +145,24 @@ def tile_metalstmcell_pa_e_kernel(tc, src_x, zx, dx_w, w_x_words, w_x_scales, ou
             ]
 
             def keep_bank(bank):
-                nc.vector.tensor_copy(
+                copy = nc.scalar.copy if bt % 2 == 0 else nc.vector.tensor_copy
+                copy(
                     out=x_grouped[bt][:].bitcast(F32).rearrange("p (c r u) -> p c r u", c=PASSES, u=2),
                     in_=bank[:].rearrange("p (c u) r -> p c r u", u=2),
                 )
+
+            return blocks, keep_bank
+
+        def then_quantise(flip, bt):
+            blocks, keep_bank = flip
+
+            def keep_bank_and_quantise(bank):
+                keep_bank(bank)
                 nc.vector.quantize_mx(
                     out=x_codes[bt][:].bitcast(FP8X4), scales=x_scales[bt][:], in_=x_grouped[bt][:]
                 )
 
-            return blocks, keep_bank
+            return blocks, keep_bank_and_quantise
 
         def flip_of_piece(g, i):
             words = piece_raw[g][i][:].bitcast(F32)
@@ -162,8 +189,9 @@ def tile_metalstmcell_pa_e_kernel(tc, src_x, zx, dx_w, w_x_words, w_x_scales, ou
         def plain_run(g, r, flips):
             for i, (hh, bt) in enumerate(banks_of_run(r)):
                 d_acc = psum.tile([P, BANK], F32, name="d_acc", tag="bank")
-                if i < len(flips):
-                    blocks, keep_bank = flips[i]
+                flip = flips[i] if i < len(flips) else None
+                if flip is not None:
+                    blocks, keep_bank = flip
                     bank = psum.tile([P, BLOCKS, P], F32, name="flip_bank", tag="bank")
                 for e in range(PAIR):
                     nc.tensor.matmul(
@@ -173,11 +201,11 @@ def tile_metalstmcell_pa_e_kernel(tc, src_x, zx, dx_w, w_x_words, w_x_scales, ou
                         start=(e == 0),
                         stop=(e == PAIR - 1),
                     )
-                    if i < len(flips):
+                    if flip is not None:
                         transposes(bank, blocks, (2 * e, 2 * e + 1))
                 d_x[(g, hh, bt)] = d_pool.tile([P, BANK], F32, name="d_x")
                 nc.scalar.copy(out=d_x[(g, hh, bt)][:], in_=d_acc[:])
-                if i < len(flips):
+                if flip is not None:
                     keep_bank(bank)
 
         def mx_run(g, r):
@@ -207,26 +235,35 @@ def tile_metalstmcell_pa_e_kernel(tc, src_x, zx, dx_w, w_x_words, w_x_scales, ou
                 nc.tensor.matmul(warm_bank[:], lhsT=warm[:, 0:P], rhs=warm[:], start=True, stop=True)
 
         warm_up(WARM_FIRST)
-        for i in (DXW_LOW, ZX):
-            blocks, keep_bank = flip_of_piece(0, i)
+        for i, first, count, copy in FIRST_PARTS:
+            words = piece_raw[0][i][:].bitcast(F32)
             bank = psum.tile([P, BLOCKS, P], F32, name="flip_bank", tag="bank")
-            transposes(bank, blocks, range(BLOCKS))
-            keep_bank(bank)
-            warm_up(WARM_BETWEEN)
+            for j in range(count):
+                nc.tensor.transpose(bank[:, j, :], words[:, first + j, :], ident[:])
+            (nc.scalar.copy if copy == "scalar" else nc.vector.tensor_copy)(
+                out=piece_flipped[0][i][:, first * P : (first + count) * P, :]
+                .rearrange("p r e -> p (r e)")
+                .bitcast(F32),
+                in_=bank[:, 0:count, :].rearrange("p j r -> p (j r)"),
+            )
+            if (i, first) == (ZX, 0):
+                warm_up(WARM_BETWEEN)
         early = (
-            [flip_of_piece(0, DXW_HIGH)]
-            + [flip_of_x(bt) for bt in range(BATCH_TILES)]
-            + [flip_of_piece(1, DXW_LOW), flip_of_piece(1, ZX)]
+            [None, flip_of_piece(0, DXW_HIGH), flip_of_x(0)]
+            + [then_quantise(flip_of_x(bt), bt - 1) for bt in range(1, EARLY_X)]
+            + [then_quantise(flip_of_piece(1, DXW_LOW), EARLY_X - 1), flip_of_piece(1, ZX)]
         )
         for r in range(RUNS):
             plain_run(0, r, early[r * RUN : (r + 1) * RUN])
-        later = [flip_of_piece(1, DXW_HIGH)] + [
-            flip_of_piece(g, i) for g in range(2, GATES) for i in range(PIECES)
-        ]
+        later = (
+            [[flip_of_x(EARLY_X)] + [then_quantise(flip_of_x(bt), bt - 1) for bt in range(EARLY_X + 1, BATCH_TILES)]]
+            + [[then_quantise(flip_of_piece(1, DXW_HIGH), BATCH_TILES - 1)]]
+            + [[flip_of_piece(g, i)] for g in range(2, GATES) for i in range(PIECES)]
+        )
         done = 0
         for g in range(GATES):
             for r in range(RUNS):
-                mx_run(g, r)
+                mx_run(g, (r % HALVES) * HALVES + r // HALVES if g == 0 else r)
                 if g + 1 < GATES:
-                    plain_run(g + 1, r, later[done : done + 1])
+                    plain_run(g + 1, r, later[done] if done < len(later) else [])
                     done += 1

@@ -31,8 +31,9 @@ FIRST_PARTS = (
     (DXW_LOW, 0, 2, "vector"),
     (DXW_LOW, 2, 2, "scalar"),
     (ZX, 0, 1, "vector"),
-    (ZX, 1, 3, "vector"),
+    (ZX, 1, 1, "vector"),
 )
+WOVEN_PART = (ZX, 2, 2, "vector")
 
 FLOPS = 2 * BATCH * GATES * H * (IN + Z)
 
@@ -113,7 +114,7 @@ def tile_metalstmcell_pa_e_kernel(tc, src_x, zx, dx_w, w_x_words, w_x_scales, ou
         def load_x(bt):
             nc.sync.dma_start(out=x_raw[bt][:], in_=src_x[bt * P : (bt + 1) * P, :])
 
-        for i, first, count, copy in FIRST_PARTS:
+        for i, first, count, copy in FIRST_PARTS + (WOVEN_PART,):
             load_piece(0, i, first, count)
         load_piece(0, DXW_HIGH)
         for bt in range(EARLY_X):
@@ -153,16 +154,19 @@ def tile_metalstmcell_pa_e_kernel(tc, src_x, zx, dx_w, w_x_words, w_x_scales, ou
 
             return blocks, keep_bank
 
-        def then_quantise(flip, bt):
-            blocks, keep_bank = flip
+        def flips_of_x_pair(bt):
+            blocks, keep_bank = flip_of_x(bt + 1)
 
             def keep_bank_and_quantise(bank):
                 keep_bank(bank)
-                nc.vector.quantize_mx(
-                    out=x_codes[bt][:].bitcast(FP8X4), scales=x_scales[bt][:], in_=x_grouped[bt][:]
-                )
+                for both in (bt, bt + 1):
+                    nc.vector.quantize_mx(
+                        out=x_codes[both][:].bitcast(FP8X4),
+                        scales=x_scales[both][:],
+                        in_=x_grouped[both][:],
+                    )
 
-            return blocks, keep_bank_and_quantise
+            return [flip_of_x(bt), (blocks, keep_bank_and_quantise)]
 
         def flip_of_piece(g, i):
             words = piece_raw[g][i][:].bitcast(F32)
@@ -172,6 +176,20 @@ def tile_metalstmcell_pa_e_kernel(tc, src_x, zx, dx_w, w_x_words, w_x_scales, ou
                 nc.vector.tensor_copy(
                     out=piece_flipped[g][i][:].rearrange("p r e -> p (r e)"),
                     in_=bank[:].rearrange("p j r -> p (j r)").bitcast(BF16),
+                )
+
+            return blocks, keep_bank
+
+        def flip_of_part(i, first, count, copy):
+            words = piece_raw[0][i][:].bitcast(F32)
+            blocks = [words[:, first + j, :] for j in range(count)]
+
+            def keep_bank(bank):
+                (nc.scalar.copy if copy == "scalar" else nc.vector.tensor_copy)(
+                    out=piece_flipped[0][i][:, first * P : (first + count) * P, :]
+                    .rearrange("p r e -> p (r e)")
+                    .bitcast(F32),
+                    in_=bank[:, 0:count, :].rearrange("p j r -> p (j r)"),
                 )
 
             return blocks, keep_bank
@@ -202,7 +220,8 @@ def tile_metalstmcell_pa_e_kernel(tc, src_x, zx, dx_w, w_x_words, w_x_scales, ou
                         stop=(e == PAIR - 1),
                     )
                     if flip is not None:
-                        transposes(bank, blocks, (2 * e, 2 * e + 1))
+                        share = len(blocks) // PAIR
+                        transposes(bank, blocks, range(share * e, share * (e + 1)))
                 d_x[(g, hh, bt)] = d_pool.tile([P, BANK], F32, name="d_x")
                 nc.scalar.copy(out=d_x[(g, hh, bt)][:], in_=d_acc[:])
                 if flip is not None:
@@ -235,29 +254,23 @@ def tile_metalstmcell_pa_e_kernel(tc, src_x, zx, dx_w, w_x_words, w_x_scales, ou
                 nc.tensor.matmul(warm_bank[:], lhsT=warm[:, 0:P], rhs=warm[:], start=True, stop=True)
 
         warm_up(WARM_FIRST)
-        for i, first, count, copy in FIRST_PARTS:
-            words = piece_raw[0][i][:].bitcast(F32)
+        for part in FIRST_PARTS:
+            blocks, keep_bank = flip_of_part(*part)
             bank = psum.tile([P, BLOCKS, P], F32, name="flip_bank", tag="bank")
-            for j in range(count):
-                nc.tensor.transpose(bank[:, j, :], words[:, first + j, :], ident[:])
-            (nc.scalar.copy if copy == "scalar" else nc.vector.tensor_copy)(
-                out=piece_flipped[0][i][:, first * P : (first + count) * P, :]
-                .rearrange("p r e -> p (r e)")
-                .bitcast(F32),
-                in_=bank[:, 0:count, :].rearrange("p j r -> p (j r)"),
-            )
-            if (i, first) == (ZX, 0):
+            transposes(bank, blocks, range(len(blocks)))
+            keep_bank(bank)
+            if part[0:2] == (ZX, 0):
                 warm_up(WARM_BETWEEN)
         early = (
-            [None, flip_of_piece(0, DXW_HIGH), flip_of_x(0)]
-            + [then_quantise(flip_of_x(bt), bt - 1) for bt in range(1, EARLY_X)]
-            + [then_quantise(flip_of_piece(1, DXW_LOW), EARLY_X - 1), flip_of_piece(1, ZX)]
+            [flip_of_part(*WOVEN_PART), flip_of_piece(0, DXW_HIGH)]
+            + flips_of_x_pair(0)
+            + [flip_of_piece(1, DXW_LOW), flip_of_piece(1, ZX)]
         )
         for r in range(RUNS):
             plain_run(0, r, early[r * RUN : (r + 1) * RUN])
         later = (
-            [[flip_of_x(EARLY_X)] + [then_quantise(flip_of_x(bt), bt - 1) for bt in range(EARLY_X + 1, BATCH_TILES)]]
-            + [[then_quantise(flip_of_piece(1, DXW_HIGH), BATCH_TILES - 1)]]
+            [flips_of_x_pair(EARLY_X)]
+            + [[flip_of_piece(1, DXW_HIGH)]]
             + [[flip_of_piece(g, i)] for g in range(2, GATES) for i in range(PIECES)]
         )
         done = 0

@@ -49,6 +49,7 @@ def tile_metalstmcell_pa_e_kernel(tc, src_x, zx, dx_w, w_x_words, w_x_scales, ou
 
         ident = keep.tile([P, P], F32, name="ident")
         x_raw = [keep.tile([P, IN], BF16, name="x_raw%d" % bt) for bt in range(BATCH_TILES)]
+        x_sorted = [keep.tile([P, IN], BF16, name="x_sorted%d" % bt) for bt in range(BATCH_TILES)]
         x_grouped = [
             keep.tile([P, PASSES * P * 4], BF16, name="x_grouped%d" % bt, align_bytes=64)
             for bt in range(BATCH_TILES)
@@ -137,13 +138,22 @@ def tile_metalstmcell_pa_e_kernel(tc, src_x, zx, dx_w, w_x_words, w_x_scales, ou
         load_words(2)
         load_words(3)
 
+        def then_sort_x(flip, tiles):
+            blocks, keep_bank = flip
+
+            def keep_bank_and_sort(bank):
+                keep_bank(bank)
+                for bt in tiles:
+                    nc.vector.tensor_copy(
+                        out=x_sorted[bt][:].bitcast(F32).rearrange("r (c u p) -> r c u p", c=PASSES, u=2),
+                        in_=x_raw[bt][:].bitcast(F32).rearrange("r (c p u) -> r c u p", c=PASSES, u=2),
+                    )
+
+            return blocks, keep_bank_and_sort
+
         def flip_of_x(bt):
-            words = x_raw[bt][:].bitcast(F32)
-            blocks = [
-                words[:, c * (K_PASS // PAIR) + u : (c + 1) * (K_PASS // PAIR) : 2]
-                for c in range(PASSES)
-                for u in range(2)
-            ]
+            words = x_sorted[bt][:].bitcast(F32)
+            blocks = [words[:, j * P : (j + 1) * P] for j in range(BLOCKS)]
 
             def keep_bank(bank):
                 copy = nc.scalar.copy if bt % 2 == 0 else nc.vector.tensor_copy
@@ -262,9 +272,9 @@ def tile_metalstmcell_pa_e_kernel(tc, src_x, zx, dx_w, w_x_words, w_x_scales, ou
             if part[0:2] == (ZX, 0):
                 warm_up(WARM_BETWEEN)
         early = (
-            [flip_of_part(*WOVEN_PART), flip_of_piece(0, DXW_HIGH)]
+            [then_sort_x(flip_of_part(*WOVEN_PART), (0,)), then_sort_x(flip_of_piece(0, DXW_HIGH), (1,))]
             + flips_of_x_pair(0)
-            + [flip_of_piece(1, DXW_LOW), flip_of_piece(1, ZX)]
+            + [flip_of_piece(1, DXW_LOW), then_sort_x(flip_of_piece(1, ZX), (2, 3))]
         )
         for r in range(RUNS):
             plain_run(0, r, early[r * RUN : (r + 1) * RUN])

@@ -89,9 +89,10 @@ def tile_metalstmcell_pa_e_kernel(tc, src_x, zx, dx_w, w_x_words, w_x_scales, ou
 
         def load_piece(g, i, first=0, count=BLOCKS):
             rows = zx[:, g, :] if i == ZX else dx_w[g, (i // 2) * BANK : (i // 2 + 1) * BANK, :]
+            rows = rows[first * P : (first + count) * P, :]
             nc.sync.dma_start(
                 out=piece_raw[g][i][:, first : first + count, :],
-                in_=rows.rearrange("(j p) z -> p j z", p=P)[:, first : first + count, :],
+                in_=rows.rearrange("(j p) z -> p j z" if i == ZX else "(p j) z -> p j z", p=P),
             )
 
         scale_rows = w_x_scales.bitcast(I32).rearrange("c q n -> q c n")
@@ -178,15 +179,23 @@ def tile_metalstmcell_pa_e_kernel(tc, src_x, zx, dx_w, w_x_words, w_x_scales, ou
 
             return [flip_of_x(bt), (blocks, keep_bank_and_quantise)]
 
+        def keep_flipped(copy, bank, g, i, first, count):
+            flipped = piece_flipped[g][i][:, first * P : (first + count) * P, :]
+            flipped = flipped.rearrange("q r e -> q (r e)").bitcast(F32)
+            if i == ZX:
+                copy(out=flipped, in_=bank[:, 0:count, :].rearrange("q j p -> q (j p)"))
+            else:
+                copy(
+                    out=flipped.rearrange("q (p j) -> q p j", j=count),
+                    in_=bank[:, 0:count, :].rearrange("q j p -> q p j"),
+                )
+
         def flip_of_piece(g, i):
             words = piece_raw[g][i][:].bitcast(F32)
             blocks = [words[:, j, :] for j in range(BLOCKS)]
 
             def keep_bank(bank):
-                nc.vector.tensor_copy(
-                    out=piece_flipped[g][i][:].rearrange("p r e -> p (r e)"),
-                    in_=bank[:].rearrange("p j r -> p (j r)").bitcast(BF16),
-                )
+                keep_flipped(nc.vector.tensor_copy, bank, g, i, 0, BLOCKS)
 
             return blocks, keep_bank
 
@@ -195,12 +204,8 @@ def tile_metalstmcell_pa_e_kernel(tc, src_x, zx, dx_w, w_x_words, w_x_scales, ou
             blocks = [words[:, first + j, :] for j in range(count)]
 
             def keep_bank(bank):
-                (nc.scalar.copy if copy == "scalar" else nc.vector.tensor_copy)(
-                    out=piece_flipped[0][i][:, first * P : (first + count) * P, :]
-                    .rearrange("p r e -> p (r e)")
-                    .bitcast(F32),
-                    in_=bank[:, 0:count, :].rearrange("p j r -> p (j r)"),
-                )
+                engine_copy = nc.scalar.copy if copy == "scalar" else nc.vector.tensor_copy
+                keep_flipped(engine_copy, bank, 0, i, first, count)
 
             return blocks, keep_bank
 

@@ -83,9 +83,9 @@ def tile_metalstmcell_pa_e_kernel(tc, src_x, zx, dx_w, w_x_words, w_x_scales, ou
 
         warm = keep.tile([P, BANK], BF16, name="warm")
         nc.vector.memset(warm[:], 0.0)
-        for g in range(GATES):
-            nc.vector.memset(w_scales[g][:].bitcast(I32), 0)
         make_identity(nc, ident[:])
+        for g in range(GATES):
+            nc.gpsimd.memset(w_scales[g][:].bitcast(F32), 0.0)
 
         def load_piece(g, i, first=0, count=BLOCKS):
             rows = zx[:, g, :] if i == ZX else dx_w[g, (i // 2) * BANK : (i // 2 + 1) * BANK, :]

from contextlib import ExitStack

import concourse.mybir as mybir
from concourse.masks import make_identity

F32 = mybir.dt.float32
BF16 = mybir.dt.bfloat16
I32 = mybir.dt.int32
U32 = mybir.dt.uint32
U8 = mybir.dt.uint8
FP8X4 = mybir.dt.float8_e4m3fn_x4
FP4X4 = mybir.dt.float4_e2m1fn_x4

P = 128
BATCH, IN, H, Z, GATES = 512, 1024, 1024, 256, 4
BATCH_TILES = BATCH // P
K_PASS = 4 * P
PASSES = IN // K_PASS
BANK = 512
HALVES = H // BANK
RUN = 2
RUNS = HALVES * BATCH_TILES // RUN
PAIR = 2
BLOCKS = 4
DXW_LOW, ZX, DXW_HIGH = 0, 1, 2
PIECES = 3
EARLY_X = 2
WARM_FIRST = 3
WARM_BETWEEN = 1
FIRST_PARTS = (
    (DXW_LOW, 0, 2, "vector"),
    (DXW_LOW, 2, 2, "scalar"),
    (ZX, 0, 1, "vector"),
    (ZX, 1, 1, "vector"),
)
WOVEN_PART = (ZX, 2, 2, "vector")

FLOPS = 2 * BATCH * GATES * H * (IN + Z)


def tile_metalstmcell_pa_e_kernel(tc, src_x, zx, dx_w, w_x_words, w_x_scales, out):
    nc = tc.nc
    with ExitStack() as ctx:
        ctx.enter_context(tc.manual_schedule())
        keep = ctx.enter_context(tc.tile_pool(name="keep", bufs=1))
        d_pool = ctx.enter_context(tc.tile_pool(name="d_pool", bufs=(RUNS + 2) * RUN))
        res_pool = ctx.enter_context(tc.tile_pool(name="res_pool", bufs=16))
        psum = ctx.enter_context(tc.psum_pool(name="psum", bufs=8))

        ident = keep.tile([P, P], F32, name="ident")
        x_raw = [keep.tile([P, IN], BF16, name="x_raw%d" % bt) for bt in range(BATCH_TILES)]
        x_sorted = [keep.tile([P, IN], BF16, name="x_sorted%d" % bt) for bt in range(BATCH_TILES)]
        x_grouped = [
            keep.tile([P, PASSES * P * 4], BF16, name="x_grouped%d" % bt, align_bytes=64)
            for bt in range(BATCH_TILES)
        ]
        x_codes = [
            keep.tile([P, PASSES * P], U32, name="x_codes%d" % bt, align_bytes=64)
            for bt in range(BATCH_TILES)
        ]
        x_scales = [
            keep.tile([P, PASSES * P], U8, name="x_scales%d" % bt, align_bytes=64)
            for bt in range(BATCH_TILES)
        ]
        piece_raw = [
            [keep.tile([P, BLOCKS, Z], BF16, name="piece_raw%d_%d" % (g, i)) for i in range(PIECES)]
            for g in range(GATES)
        ]
        piece_flipped = [
            [
                keep.tile([P, BLOCKS * P, PAIR], BF16, name="piece_flipped%d_%d" % (g, i))
                for i in range(PIECES)
            ]
            for g in range(GATES)
        ]
        w_words = [
            keep.tile([P, PASSES, 2 * H], U8, name="w_words%d" % g, align_bytes=64)
            for g in range(GATES)
        ]
        w_scales = [
            keep.tile([P, PASSES, H], U8, name="w_scales%d" % g, align_bytes=64) for g in range(GATES)
        ]

        warm = keep.tile([P, BANK], BF16, name="warm")
        nc.vector.memset(warm[:], 0.0)
        make_identity(nc, ident[:])
        for g in range(GATES):
            nc.gpsimd.memset(w_scales[g][:].bitcast(F32), 0.0)

        def load_piece(g, i, first=0, count=BLOCKS):
            rows = zx[:, g, :] if i == ZX else dx_w[g, (i // 2) * BANK : (i // 2 + 1) * BANK, :]
            rows = rows[first * P : (first + count) * P, :]
            nc.sync.dma_start(
                out=piece_raw[g][i][:, first : first + count, :],
                in_=rows.rearrange("(j p) z -> p j z" if i == ZX else "(p j) z -> p j z", p=P),
            )

        scale_rows = w_x_scales.bitcast(I32).rearrange("c q n -> q c n")

        def load_scales(g):
            for r in range(4):
                nc.sync.dma_start(
                    out=w_scales[g][:].bitcast(I32)[r : P : 32],
                    in_=scale_rows[r : 16 : 4, g * PASSES : (g + 1) * PASSES],
                )

        def load_words(g, first_half=0, halves=HALVES):
            low, high = first_half * BANK // 2, (first_half + halves) * BANK // 2
            nc.sync.dma_start(
                out=w_words[g][:].bitcast(I32)[:, :, low:high],
                in_=w_x_words.bitcast(I32)[g * PASSES : (g + 1) * PASSES, :, low:high].rearrange(
                    "c p n -> p c n"
                ),
            )

        def load_x(bt):
            nc.sync.dma_start(out=x_raw[bt][:], in_=src_x[bt * P : (bt + 1) * P, :])

        for i, first, count, copy in FIRST_PARTS + (WOVEN_PART,):
            load_piece(0, i, first, count)
        load_piece(0, DXW_HIGH)
        for bt in range(EARLY_X):
            load_x(bt)
        load_piece(1, DXW_LOW)
        load_piece(1, ZX)
        load_scales(0)
        for hh in range(HALVES):
            load_words(0, hh, 1)
        for bt in range(EARLY_X, BATCH_TILES):
            load_x(bt)
        load_piece(1, DXW_HIGH)
        for i in range(PIECES):
            load_piece(2, i)
        for g in range(1, GATES):
            load_scales(g)
        load_words(1)
        for i in range(PIECES):
            load_piece(3, i)
        load_words(2)
        load_words(3)

        def then_sort_x(flip, tiles):
            blocks, keep_bank = flip

            def keep_bank_and_sort(bank):
                keep_bank(bank)
                for bt in tiles:
                    nc.vector.tensor_copy(
                        out=x_sorted[bt][:].bitcast(F32).rearrange("r (c u p) -> r c u p", c=PASSES, u=2),
                        in_=x_raw[bt][:].bitcast(F32).rearrange("r (c p u) -> r c u p", c=PASSES, u=2),
                    )

            return blocks, keep_bank_and_sort

        def flip_of_x(bt):
            words = x_sorted[bt][:].bitcast(F32)
            blocks = [words[:, j * P : (j + 1) * P] for j in range(BLOCKS)]

            def keep_bank(bank):
                copy = nc.scalar.copy if bt % 2 == 0 else nc.vector.tensor_copy
                copy(
                    out=x_grouped[bt][:].bitcast(F32).rearrange("p (c r u) -> p c r u", c=PASSES, u=2),
                    in_=bank[:].rearrange("p (c u) r -> p c r u", u=2),
                )

            return blocks, keep_bank

        def flips_of_x_pair(bt):
            blocks, keep_bank = flip_of_x(bt + 1)

            def keep_bank_and_quantise(bank):
                keep_bank(bank)
                for both in (bt, bt + 1):
                    nc.vector.quantize_mx(
                        out=x_codes[both][:].bitcast(FP8X4),
                        scales=x_scales[both][:],
                        in_=x_grouped[both][:],
                    )

            return [flip_of_x(bt), (blocks, keep_bank_and_quantise)]

        def keep_flipped(copy, bank, g, i, first, count):
            flipped = piece_flipped[g][i][:, first * P : (first + count) * P, :]
            flipped = flipped.rearrange("q r e -> q (r e)").bitcast(F32)
            if i == ZX:
                copy(out=flipped, in_=bank[:, 0:count, :].rearrange("q j p -> q (j p)"))
            else:
                copy(
                    out=flipped.rearrange("q (p j) -> q p j", j=count),
                    in_=bank[:, 0:count, :].rearrange("q j p -> q p j"),
                )

        def flip_of_piece(g, i):
            words = piece_raw[g][i][:].bitcast(F32)
            blocks = [words[:, j, :] for j in range(BLOCKS)]

            def keep_bank(bank):
                keep_flipped(nc.vector.tensor_copy, bank, g, i, 0, BLOCKS)

            return blocks, keep_bank

        def flip_of_part(i, first, count, copy):
            words = piece_raw[0][i][:].bitcast(F32)
            blocks = [words[:, first + j, :] for j in range(count)]

            def keep_bank(bank):
                engine_copy = nc.scalar.copy if copy == "scalar" else nc.vector.tensor_copy
                keep_flipped(engine_copy, bank, 0, i, first, count)

            return blocks, keep_bank

        def transposes(bank, blocks, which):
            for j in which:
                nc.tensor.transpose(bank[:, j, :], blocks[j], ident[:])

        def banks_of_run(r):
            hh, group = divmod(r, BATCH_TILES // RUN)
            return [(hh, group * RUN + i) for i in range(RUN)]

        d_x = {}

        def plain_run(g, r, flips):
            for i, (hh, bt) in enumerate(banks_of_run(r)):
                d_acc = psum.tile([P, BANK], F32, name="d_acc", tag="bank")
                flip = flips[i] if i < len(flips) else None
                if flip is not None:
                    blocks, keep_bank = flip
                    bank = psum.tile([P, BLOCKS, P], F32, name="flip_bank", tag="bank")
                for e in range(PAIR):
                    nc.tensor.matmul(
                        d_acc[:],
                        lhsT=piece_flipped[g][ZX][:, bt * P : (bt + 1) * P, e],
                        rhs=piece_flipped[g][2 * hh][:, :, e],
                        start=(e == 0),
                        stop=(e == PAIR - 1),
                    )
                    if flip is not None:
                        share = len(blocks) // PAIR
                        transposes(bank, blocks, range(share * e, share * (e + 1)))
                d_x[(g, hh, bt)] = d_pool.tile([P, BANK], F32, name="d_x")
                nc.scalar.copy(out=d_x[(g, hh, bt)][:], in_=d_acc[:])
                if flip is not None:
                    keep_bank(bank)

        def mx_run(g, r):
            for hh, bt in banks_of_run(r):
                cols = slice(hh * BANK, (hh + 1) * BANK)
                w_acc = psum.tile([P, BANK], F32, name="w_acc", tag="bank")
                for c in range(PASSES):
                    nc.tensor.matmul_mx(
                        out=w_acc[:],
                        lhsT=x_codes[bt][:, c * P : (c + 1) * P].bitcast(FP8X4),
                        lhsT_scale=x_scales[bt][:, c * P : (c + 1) * P],
                        rhs=w_words[g][:, c, 2 * hh * BANK : 2 * (hh + 1) * BANK].bitcast(FP4X4),
                        rhs_scale=w_scales[g][:, c, cols],
                        start=(c == 0),
                        stop=(c == PASSES - 1),
                    )
                res = res_pool.tile([P, BANK], F32, name="res")
                nc.vector.tensor_tensor(
                    out=res[:], in0=w_acc[:], in1=d_x[(g, hh, bt)][:], op=mybir.AluOpType.mult
                )
                nc.sync.dma_start(out=out[bt * P : (bt + 1) * P, g, cols], in_=res[:])

        warm_bank = psum.tile([P, BANK], F32, name="warm_bank", tag="bank")

        def warm_up(n):
            for i_warm in range(n):
                nc.tensor.matmul(warm_bank[:], lhsT=warm[:, 0:P], rhs=warm[:], start=True, stop=True)

        warm_up(WARM_FIRST)
        for part in FIRST_PARTS:
            blocks, keep_bank = flip_of_part(*part)
            bank = psum.tile([P, BLOCKS, P], F32, name="flip_bank", tag="bank")
            transposes(bank, blocks, range(len(blocks)))
            keep_bank(bank)
            if part[0:2] == (ZX, 0):
                warm_up(WARM_BETWEEN)
        early = (
            [then_sort_x(flip_of_part(*WOVEN_PART), (0,)), then_sort_x(flip_of_piece(0, DXW_HIGH), (1,))]
            + flips_of_x_pair(0)
            + [flip_of_piece(1, DXW_LOW), then_sort_x(flip_of_piece(1, ZX), (2, 3))]
        )
        for r in range(RUNS):
            plain_run(0, r, early[r * RUN : (r + 1) * RUN])
        later = (
            [flips_of_x_pair(EARLY_X)]
            + [[flip_of_piece(1, DXW_HIGH)]]
            + [[flip_of_piece(g, i)] for g in range(2, GATES) for i in range(PIECES)]
        )
        done = 0
        for g in range(GATES):
            for r in range(RUNS):
                mx_run(g, (r % HALVES) * HALVES + r // HALVES if g == 0 else r)
                if g + 1 < GATES:
                    plain_run(g + 1, r, later[done] if done < len(later) else [])
                    done += 1
